import numpy as np
import ml_dtypes


def mxq(x, axis, fmt="e4m3"):
    dtype, down = {"e4m3": (ml_dtypes.float8_e4m3fn, 7), "e5m2": (ml_dtypes.float8_e5m2, 14)}[fmt]
    v = np.moveaxis(np.asarray(x, np.float32).astype(ml_dtypes.bfloat16).astype(np.float64), axis, -1)
    blocks = v.reshape(v.shape[:-1] + (-1, 32))
    amax = np.abs(blocks).max(-1, keepdims=True)
    byte = np.maximum(np.where(amax > 0, np.frexp(amax)[1] - 1 + 127, 0) - down, 1)
    scale = np.exp2(byte - 127.0)
    codes = (blocks / scale).astype(np.float32).astype(dtype).astype(np.float64)
    return np.moveaxis((codes * scale).reshape(v.shape), -1, axis)


WIDE = False


def mx_kscale(k):
    if not WIDE:
        return np.ones(k)
    levels = np.array([10, -10, 5, -5, 0])
    a = np.random.permutation(np.resize(levels, k // 512 * 4)).reshape(k // 512, 4)
    idx = np.arange(k)
    return np.exp2(a[idx // 512, idx % 128 // 32])


BF16 = ml_dtypes.bfloat16


def bf(x):
    return np.asarray(x, np.float32).astype(BF16)


def f64(x):
    return np.asarray(x).astype(np.float64)


N, D_IN, H0, H1, K = 1024, 3072, 1024, 256, 20
V = 1.0


def silu(v):
    return v / (1.0 + np.exp(-v))


def setup_inputs():
    s = mx_kscale(D_IN)
    w1 = np.random.standard_normal((D_IN, H0)) / np.sqrt(D_IN)
    b1 = np.random.standard_normal(H0) * 0.2
    w2 = np.random.standard_normal((H0, H1)) * 4.0 / np.sqrt(H0 * H1)
    b2 = np.random.standard_normal(H1) * 0.1
    cent = np.random.standard_normal((K, D_IN)) * 0.9
    x = cent[np.random.randint(0, K, N)] + np.random.standard_normal((N, D_IN)) * 0.44
    hc = silu(np.stack([(c[:, None] * w1).sum(0) for c in cent]) + b1)
    clusters = (hc[:, :, None] * w2[None]).sum(1) + b2 + np.random.standard_normal((K, H1)) * 0.5 / np.sqrt(H1)
    return {"x": bf(x * s), "W1": bf(w1 / s[:, None]), "b1": bf(b1), "W2": bf(w2), "b2": bf(b2), "clusters": bf(clusters)}


def reference(x, W1, b1, W2, b2, clusters):
    h = silu((mxq(f64(x), 1, "e4m3") @ mxq(f64(W1), 0, "e4m3")) + f64(b1))
    z = (mxq(h, 1, "e4m3") @ mxq(f64(W2), 0, "e4m3")) + f64(b2)
    d2 = np.stack([((z - c) ** 2).sum(1) for c in f64(clusters)], axis=1)
    q = 1.0 / (1.0 + d2 / V)
    q = q ** ((V + 1.0) / 2.0)
    q = q / q.sum(1, keepdims=True)
    return z, q

@@ -1,0 +1,404 @@
+from contextlib import ExitStack
+
+import concourse.mybir as mybir
+from concourse.masks import make_identity
+
+F32 = mybir.dt.float32
+BF16 = mybir.dt.bfloat16
+U32 = mybir.dt.uint32
+U8 = mybir.dt.uint8
+FP8X4 = mybir.dt.float8_e4m3fn_x4
+AF = mybir.ActivationFunctionType
+ALU = mybir.AluOpType
+AX = mybir.AxisListType
+
+P = 128
+N_ROWS, D_IN, H0, H1, NCL = 1024, 3072, 1024, 256, 20
+G1 = D_IN // 512
+G2 = H0 // 512
+MT = H0 // P
+FLOPS = 2 * N_ROWS * D_IN * H0 + 2 * N_ROWS * H0 * H1 + 3 * N_ROWS * H1 * NCL
+
+PIN = True
+CO_ON_VECTOR = (4, 9, 14, 19, 22)
+XR_BUFS = 5
+EARLY_AFTER = 6
+N_EARLY = 1
+WR_BUFS = 6
+
+
+def tile_lintrans_pa_kernel(tc, x, W1, b1, W2, b2, clusters, out_0, out_1):
+    nc = tc.nc
+    with ExitStack() as ctx:
+        if PIN:
+            ctx.enter_context(tc.manual_schedule())
+        const = ctx.enter_context(tc.tile_pool(name="const", bufs=1))
+        keep = ctx.enter_context(tc.tile_pool(name="keep", bufs=1))
+        xraw = ctx.enter_context(tc.tile_pool(name="xraw", bufs=XR_BUFS))
+        wraw = ctx.enter_context(tc.tile_pool(name="wraw", bufs=WR_BUFS))
+        xgp = ctx.enter_context(tc.tile_pool(name="xgp", bufs=6))
+        wgp = ctx.enter_context(tc.tile_pool(name="wgp", bufs=3))
+        hgp = ctx.enter_context(tc.tile_pool(name="hgp", bufs=2))
+        small = ctx.enter_context(tc.tile_pool(name="small", bufs=2))
+        psum = ctx.enter_context(tc.psum_pool(name="psum", bufs=1))
+
+        bank_no = [0]
+
+        def new_bank(dtype=F32, cols=512):
+            k = bank_no[0] % 8
+            bank_no[0] += 1
+            return psum.tile([P, cols], dtype, tag="bank%d" % k, name="bank%d" % k)
+
+        x_view = x.rearrange("(p i) k -> p i k", i=8)
+        z_view = out_0.rearrange("(p i) j -> p i j", i=8)
+        q_view = out_1.rearrange("(p i) k -> p i k", i=8)
+
+        ident_f = const.tile([P, P], F32, name="ident_f")
+        make_identity(nc, ident_f[:])
+        ident_b = const.tile([P, P], BF16, name="ident_b")
+        make_identity(nc, ident_b[:])
+        misc = const.tile([P, 2 * P], BF16, name="misc")
+        nc.vector.memset(misc[:], 0.0)
+        brow = const.tile([P, H1], BF16, name="brow")
+        nc.vector.memset(brow[:], 0.0)
+        ones_f = const.tile([P, P], F32, name="ones_f")
+        nc.vector.memset(ones_f[:], 1.0)
+        ones_b = const.tile([P, P], BF16, name="ones_b")
+        nc.vector.memset(ones_b[:], 1.0)
+        warm = const.tile([P, 2], F32, name="warm")
+        nc.vector.memset(warm[:], 0.0)
+        nc.scalar.dma_start(out=misc[0:NCL, :], in_=clusters)
+        nc.scalar.dma_start(out=misc[32 : 32 + MT, 0:P], in_=b1.rearrange("(m p) -> m p", p=P))
+        nc.scalar.dma_start(out=misc[64:66, 0:P], in_=b2.rearrange("(a p) -> a p", p=P))
+        nc.scalar.dma_start(out=brow[0:1, :], in_=b2.rearrange("(o j) -> o j", o=1))
+        nc.scalar.activation(out=warm[:, 1:2], in_=warm[:, 0:1], func=AF.Silu)
+
+        xq = keep.tile([P, G1, N_ROWS], U32, name="xq", align_bytes=64)
+        xs = keep.tile([P, G1, N_ROWS], U8, name="xs", align_bytes=64)
+        wq = keep.tile([P, G1, H0], U32, name="wq", align_bytes=64)
+        ws = keep.tile([P, G1, H0], U8, name="ws", align_bytes=64)
+        h_bf = keep.tile([P, MT, N_ROWS], BF16, name="h_bf")
+        hq = keep.tile([P, G2, N_ROWS], U32, name="hq", align_bytes=64)
+        hs = keep.tile([P, G2, N_ROWS], U8, name="hs", align_bytes=64)
+        w2r = keep.tile([P, G2 * 4, H1], BF16, name="w2r")
+        w2g = keep.tile([P, G2, H1, 4], BF16, name="w2g", align_bytes=64)
+        w2q = keep.tile([P, G2, H1], U32, name="w2q", align_bytes=64)
+        w2s = keep.tile([P, G2, H1], U8, name="w2s", align_bytes=64)
+        zT_sb = keep.tile([P, 2, N_ROWS], F32, name="zT_sb")
+        z_sb = keep.tile([P, 8, H1], F32, name="z_sb")
+        q_sb = keep.tile([P, 8, NCL], F32, name="q_sb")
+        z2 = keep.tile([P, 8], F32, name="z2")
+        b1T = keep.tile([P, MT], F32, name="b1T")
+        b2T = keep.tile([P, 2], F32, name="b2T")
+        cTm2 = keep.tile([P, 2, NCL], F32, name="cTm2")
+        csq = keep.tile([P, 2, NCL], F32, name="csq")
+        cc1 = keep.tile([P, NCL], F32, name="cc1")
+        b2bc = keep.tile([P, H1], F32, name="b2bc")
+
+        xr = {}
+        wr = {}
+
+        def load_x(i):
+            xr[i] = xraw.tile([P, D_IN], BF16, tag="xr", name="xr")
+            nc.sync.dma_start(out=xr[i][:], in_=x_view[:, i, :])
+
+        def load_w(side, c):
+            wr[(side, c)] = wraw.tile([P, 4, 512], BF16, tag="wr", name="wr")
+            for u in range(2):
+                rows = slice(512 * c + 256 * u, 512 * c + 256 * (u + 1))
+                nc.sync.dma_start(
+                    out=wr[(side, c)][:, 2 * u : 2 * u + 2, :],
+                    in_=W1[rows, 512 * side : 512 * (side + 1)].rearrange("(q e) w -> q e w", e=2),
+                )
+
+        def load_w2():
+            nc.sync.dma_start(out=w2r[:], in_=W2.rearrange("(a p) j -> p a j", p=P))
+
+        xg = {}
+
+        def x_transpose(i, gp):
+            u = 3 * i + gp
+            bank = new_bank()
+            words = xr[i][:].bitcast(F32)
+            for s in range(4):
+                nc.tensor.transpose(bank[:, P * s : P * (s + 1)], words[:, 512 * gp + P * s : 512 * gp + P * (s + 1)], ident_f[:])
+            xg[u] = xgp.tile([P, 1024], BF16, tag="xg", name="xg", align_bytes=64)
+            dst = xg[u][:].bitcast(F32).rearrange("p (g n u) -> p g n u", g=2, u=2)
+            src = bank[:].rearrange("p (g u n) -> p g n u", g=2, u=2)
+            if u in CO_ON_VECTOR:
+                nc.vector.tensor_copy(out=dst, in_=src)
+            else:
+                nc.scalar.copy(out=dst, in_=src)
+
+        def x_quantise(i, gp):
+            u = 3 * i + gp
+            cols = slice(P * i, P * (i + 1))
+            for g2 in range(2):
+                g = 2 * gp + g2
+                nc.vector.quantize_mx(
+                    out=xq[:, g, cols].bitcast(FP8X4), scales=xs[:, g, cols], in_=xg[u][:, 512 * g2 : 512 * (g2 + 1)]
+                )
+
+        def small_prep():
+            mt = new_bank(BF16, 2 * P)
+            for a in range(2):
+                nc.tensor.transpose(mt[:, P * a : P * (a + 1)], misc[:, P * a : P * (a + 1)], ident_b[:])
+            mview = mt[:].rearrange("p (a r) -> p a r", a=2)
+            nc.vector.tensor_scalar(out=cTm2[:], in0=mview[:, :, 0:NCL], scalar1=-2.0, scalar2=None, op0=ALU.mult)
+            nc.vector.tensor_copy(out=b1T[:], in_=mt[:, 32 : 32 + MT])
+            nc.vector.tensor_copy(out=b2T[:], in_=mt[:, 64:66])
+            nc.vector.tensor_tensor(out=csq[:], in0=cTm2[:], in1=cTm2[:], op=ALU.mult)
+
+        def small_prep2():
+            cb = new_bank()
+            nc.tensor.matmul(out=cb[:, 0:H1], lhsT=ones_b[:], rhs=brow[:], start=True, stop=True)
+            for a in range(2):
+                nc.tensor.matmul(out=cb[:, H1 : H1 + NCL], lhsT=ones_f[:], rhs=csq[:, a, :], start=(a == 0), stop=(a == 1))
+            nc.vector.tensor_copy(out=b2bc[:], in_=cb[:, 0:H1])
+            nc.vector.tensor_scalar(out=cc1[:], in0=cb[:, H1 : H1 + NCL], scalar1=0.25, scalar2=1.0, op0=ALU.mult, op1=ALU.add)
+
+        wg = {}
+
+        def regroup(engine, dst, src):
+            d = dst.rearrange("p (c i) t -> p c t i", i=4)
+            s = src.rearrange("p t (c i) -> p c t i", i=4)
+            if engine == "v":
+                nc.vector.tensor_copy(out=d, in_=s)
+            else:
+                nc.scalar.copy(out=d, in_=s)
+
+        def w_regroup(side, c, quarter, engine):
+            if (side, c) not in wg:
+                wg[(side, c)] = wgp.tile([P, 512, 4], BF16, tag="wg", name="wg", align_bytes=64)
+            cols = slice(256 * quarter, 256 * (quarter + 1))
+            regroup(engine, wg[(side, c)][:, cols, :], wr[(side, c)][:, :, cols])
+
+        def w_quantise(side, c, quarter):
+            cols = slice(256 * quarter, 256 * (quarter + 1))
+            dcols = slice(512 * side + 256 * quarter, 512 * side + 256 * (quarter + 1))
+            nc.vector.quantize_mx(
+                out=wq[:, c, dcols].bitcast(FP8X4),
+                scales=ws[:, c, dcols],
+                in_=wg[(side, c)][:, cols, :].rearrange("p w t -> p (w t)"),
+            )
+
+        def l1_pass(acc, m, g, col0, ncols):
+            nc.tensor.matmul_mx(
+                out=acc[:, 0:ncols],
+                lhsT=wq[:, g, P * m : P * (m + 1)].bitcast(FP8X4),
+                lhsT_scale=ws[:, g, P * m : P * (m + 1)],
+                rhs=xq[:, g, col0 : col0 + ncols].bitcast(FP8X4),
+                rhs_scale=xs[:, g, col0 : col0 + ncols],
+                start=(g == 0),
+                stop=(g == G1 - 1),
+            )
+
+        def silu(acc, m, col0, ncols):
+            nc.scalar.activation(
+                out=h_bf[:, m, col0 : col0 + ncols], in_=acc[:, 0:ncols], func=AF.Silu, bias=b1T[:, m : m + 1], scale=1.0
+            )
+
+        def h_quantise(col0, ncols, gg):
+            hg = hgp.tile([P, ncols, 4], BF16, tag="hg", name="hg", align_bytes=64)
+            regroup("v", hg[:], h_bf[:, 4 * gg : 4 * (gg + 1), col0 : col0 + ncols])
+            return hg
+
+        def h_quantise2(hg, col0, ncols, gg):
+            nc.vector.quantize_mx(
+                out=hq[:, gg, col0 : col0 + ncols].bitcast(FP8X4),
+                scales=hs[:, gg, col0 : col0 + ncols],
+                in_=hg[:].rearrange("p n t -> p (n t)"),
+            )
+
+        def w2_prep():
+            for gg in range(G2):
+                regroup("v", w2g[:, gg, :, :], w2r[:, 4 * gg : 4 * (gg + 1), :])
+            nc.vector.quantize_mx(
+                out=w2q[:].rearrange("p g j -> p (g j)").bitcast(FP8X4),
+                scales=w2s[:].rearrange("p g j -> p (g j)"),
+                in_=w2g[:].rearrange("p g j t -> p (g j t)"),
+            )
+
+        def layer2(col0, ncols):
+            i0, nt = col0 // P, ncols // P
+            zt = []
+            for jt in range(2):
+                if ncols == 512 or jt == 0:
+                    bank = new_bank()
+                off = 0 if ncols == 512 else ncols * jt
+                for gg in range(G2):
+                    nc.tensor.matmul_mx(
+                        out=bank[:, off : off + ncols],
+                        lhsT=w2q[:, gg, P * jt : P * (jt + 1)].bitcast(FP8X4),
+                        lhsT_scale=w2s[:, gg, P * jt : P * (jt + 1)],
+                        rhs=hq[:, gg, col0 : col0 + ncols].bitcast(FP8X4),
+                        rhs_scale=hs[:, gg, col0 : col0 + ncols],
+                        start=(gg == 0),
+                        stop=(gg == G2 - 1),
+                    )
+                zt.append(bank[:, off : off + ncols])
+            zb = []
+            for ii in range(nt):
+                if ii % 2 == 0:
+                    bank = new_bank()
+                    zb.append(bank)
+                i = i0 + ii
+                for gg in range(G2):
+                    nc.tensor.matmul_mx(
+                        out=bank[:, H1 * (ii % 2) : H1 * (ii % 2 + 1)],
+                        lhsT=hq[:, gg, P * i : P * (i + 1)].bitcast(FP8X4),
+                        lhsT_scale=hs[:, gg, P * i : P * (i + 1)],
+                        rhs=w2q[:, gg, :].bitcast(FP8X4),
+                        rhs_scale=w2s[:, gg, :],
+                        start=(gg == 0),
+                        stop=(gg == G2 - 1),
+                    )
+            for jt in range(2):
+                nc.scalar.activation(
+                    out=zT_sb[:, jt, col0 : col0 + ncols], in_=zt[jt], func=AF.Identity, bias=b2T[:, jt : jt + 1], scale=1.0
+                )
+            for k, bank in enumerate(zb):
+                i = i0 + 2 * k
+                nc.vector.tensor_tensor(
+                    out=z_sb[:, i : i + 2, :],
+                    in0=bank[:].rearrange("p (i j) -> p i j", i=2),
+                    in1=b2bc[:].unsqueeze(1).to_broadcast([P, 2, H1]),
+                    op=ALU.add,
+                )
+            nc.sync.dma_start(out=z_view[:, i0 : i0 + nt, :], in_=z_sb[:, i0 : i0 + nt, :])
+            for ii in range(nt):
+                junk = small.tile([P, H1], F32, tag="junk", name="junk")
+                nc.scalar.activation(out=junk[:], in_=z_sb[:, i0 + ii, :], func=AF.Square, accum_out=z2[:, i0 + ii : i0 + ii + 1])
+
+        def dist(col0, ncols):
+            i0, nt = col0 // P, ncols // P
+            shape = [P, nt, NCL]
+            ee = small.tile(shape, F32, tag="ee%d" % nt, name="ee")
+            nc.vector.tensor_tensor(
+                out=ee[:],
+                in0=cc1[:].unsqueeze(1).to_broadcast(shape),
+                in1=z2[:, i0 : i0 + nt].unsqueeze(2).to_broadcast(shape),
+                op=ALU.add,
+            )
+            db = new_bank()
+            for ii in range(nt):
+                i = i0 + ii
+                for jt in range(2):
+                    nc.tensor.matmul(
+                        out=db[:, 32 * ii : 32 * ii + NCL],
+                        lhsT=zT_sb[:, jt, P * i : P * (i + 1)],
+                        rhs=cTm2[:, jt, :],
+                        start=(jt == 0),
+                        stop=(jt == 1),
+                    )
+            dview = db[:, 0 : 32 * nt].rearrange("p (i k) -> p i k", k=32)[:, :, 0:NCL]
+            dd = small.tile(shape, F32, tag="dd%d" % nt, name="dd")
+            nc.vector.tensor_tensor(out=dd[:], in0=dview, in1=ee[:], op=ALU.add)
+            tt = small.tile(shape, F32, tag="tt%d" % nt, name="tt")
+            nc.vector.reciprocal(out=tt[:], in_=dd[:])
+            sm = small.tile([P, nt], F32, tag="sm%d" % nt, name="sm")
+            nc.vector.reduce_sum(out=sm[:], in_=tt[:], axis=AX.X)
+            rs = small.tile([P, nt], F32, tag="rs%d" % nt, name="rs")
+            nc.vector.reciprocal(out=rs[:], in_=sm[:])
+            nc.vector.tensor_tensor(
+                out=q_sb[:, i0 : i0 + nt, :], in0=tt[:], in1=rs[:].unsqueeze(2).to_broadcast(shape), op=ALU.mult
+            )
+            nc.sync.dma_start(out=q_view[:, i0 : i0 + nt, :], in_=q_sb[:, i0 : i0 + nt, :])
+
+        def w_rg(side, c):
+            w_regroup(side, c, 0, "v")
+            w_regroup(side, c, 1, "s")
+
+        def w_q(side, c):
+            w_quantise(side, c, 0)
+            w_quantise(side, c, 1)
+
+        def hq_all(col0, ncols, gg):
+            hg = h_quantise(col0, ncols, gg)
+            h_quantise2(hg, col0, ncols, gg)
+
+        for i in range(XR_BUFS):
+            load_x(i)
+        units = [(i, gp) for i in range(8) for gp in range(3)]
+        for n, (i, gp) in enumerate(units):
+            x_transpose(i, gp)
+            if n >= 2:
+                x_quantise(*units[n - 2])
+            if gp == 2:
+                if i + XR_BUFS < 8:
+                    load_x(i + XR_BUFS)
+                if i + XR_BUFS == EARLY_AFTER:
+                    for c in range(N_EARLY):
+                        load_w(0, c)
+                if i + XR_BUFS == 7:
+                    for c in range(N_EARLY, G1):
+                        load_w(0, c)
+                if i == 1:
+                    small_prep()
+                if i == 6:
+                    w_rg(0, 0)
+            if (i, gp) == (7, 1):
+                w_q(0, 0)
+        x_quantise(*units[-2])
+        x_quantise(*units[-1])
+        small_prep2()
+
+        acc = {}
+        for m in range(4):
+            for b in range(2):
+                acc[(m, b)] = new_bank()
+        w_rg(0, 1)
+        for c in range(G1):
+            if 0 < c < G1 - 1:
+                w_rg(0, c + 1)
+            if c > 0:
+                w_q(0, c)
+            load_w(1, c)
+            for m in range(4):
+                for b in range(2):
+                    l1_pass(acc[(m, b)], m, c, 512 * b, 512)
+        load_w2()
+        for c in range(4):
+            w_rg(1, c)
+            w_q(1, c)
+        for m in range(2):
+            for b in range(2):
+                silu(acc[(m, b)], m, 512 * b, 512)
+        for c in range(4, G1):
+            w_rg(1, c)
+            w_q(1, c)
+        for m in range(2, 4):
+            for b in range(2):
+                silu(acc[(m, b)], m, 512 * b, 512)
+        acca = {}
+        for m in range(4, 8):
+            acca[m] = new_bank()
+        for g in range(G1):
+            for m in range(4, 8):
+                l1_pass(acca[m], m, g, 0, 512)
+        w2_prep()
+        hq_all(0, 512, 0)
+        hq_all(512, 256, 0)
+        hq_all(768, 256, 0)
+        for m in range(4, 8):
+            silu(acca[m], m, 0, 512)
+        hq_all(0, 512, 1)
+
+        def round2(col0, ncols, ms):
+            for m in ms:
+                a = new_bank()
+                for g in range(G1):
+                    l1_pass(a, m, g, col0, ncols)
+                silu(a, m, col0, ncols)
+                if m == 7:
+                    hq_all(col0, ncols, 1)
+
+        round2(512, 256, range(4, 8))
+        round2(768, 256, range(4, 6))
+        layer2(0, 512)
+        round2(768, 256, range(6, 8))
+        layer2(512, 256)
+        dist(0, 512)
+        layer2(768, 256)
+        dist(512, 256)
+        dist(768, 256)

@@ -59,18 +59,13 @@ def tile_lintrans_pa_kernel(tc, x, W1, b1, W2, b2, clusters, out_0, out_1):
         make_identity(nc, ident_b[:])
         misc = const.tile([P, 2 * P], BF16, name="misc")
         nc.vector.memset(misc[:], 0.0)
-        brow = const.tile([P, H1], BF16, name="brow")
-        nc.vector.memset(brow[:], 0.0)
         ones_f = const.tile([P, P], F32, name="ones_f")
         nc.vector.memset(ones_f[:], 1.0)
-        ones_b = const.tile([P, P], BF16, name="ones_b")
-        nc.vector.memset(ones_b[:], 1.0)
         warm = const.tile([P, 2], F32, name="warm")
         nc.vector.memset(warm[:], 0.0)
         nc.scalar.dma_start(out=misc[0:NCL, :], in_=clusters)
         nc.scalar.dma_start(out=misc[32 : 32 + MT, 0:P], in_=b1.rearrange("(m p) -> m p", p=P))
         nc.scalar.dma_start(out=misc[64:66, 0:P], in_=b2.rearrange("(a p) -> a p", p=P))
-        nc.scalar.dma_start(out=brow[0:1, :], in_=b2.rearrange("(o j) -> o j", o=1))
         nc.scalar.activation(out=warm[:, 1:2], in_=warm[:, 0:1], func=AF.Silu)
 
         xq = keep.tile([P, G1, N_ROWS], U32, name="xq", align_bytes=64)
@@ -93,7 +88,6 @@ def tile_lintrans_pa_kernel(tc, x, W1, b1, W2, b2, clusters, out_0, out_1):
         cTm2 = keep.tile([P, 2, NCL], F32, name="cTm2")
         csq = keep.tile([P, 2, NCL], F32, name="csq")
         cc1 = keep.tile([P, NCL], F32, name="cc1")
-        b2bc = keep.tile([P, H1], F32, name="b2bc")
 
         xr = {}
         wr = {}
@@ -151,10 +145,11 @@ def tile_lintrans_pa_kernel(tc, x, W1, b1, W2, b2, clusters, out_0, out_1):
 
         def small_prep2():
             cb = new_bank()
-            nc.tensor.matmul(out=cb[:, 0:H1], lhsT=ones_b[:], rhs=brow[:], start=True, stop=True)
             for a in range(2):
                 nc.tensor.matmul(out=cb[:, H1 : H1 + NCL], lhsT=ones_f[:], rhs=csq[:, a, :], start=(a == 0), stop=(a == 1))
-            nc.vector.tensor_copy(out=b2bc[:], in_=cb[:, 0:H1])
+            return cb
+
+        def small_prep3(cb):
             nc.vector.tensor_scalar(out=cc1[:], in0=cb[:, H1 : H1 + NCL], scalar1=0.25, scalar2=1.0, op0=ALU.mult, op1=ALU.add)
 
         wg = {}
@@ -237,42 +232,59 @@ def tile_lintrans_pa_kernel(tc, x, W1, b1, W2, b2, clusters, out_0, out_1):
                         stop=(gg == G2 - 1),
                     )
                 zt.append(bank[:, off : off + ncols])
-            zb = []
-            for ii in range(nt):
-                if ii % 2 == 0:
-                    bank = new_bank()
-                    zb.append(bank)
-                i = i0 + ii
-                for gg in range(G2):
-                    nc.tensor.matmul_mx(
-                        out=bank[:, H1 * (ii % 2) : H1 * (ii % 2 + 1)],
-                        lhsT=hq[:, gg, P * i : P * (i + 1)].bitcast(FP8X4),
-                        lhsT_scale=hs[:, gg, P * i : P * (i + 1)],
-                        rhs=w2q[:, gg, :].bitcast(FP8X4),
-                        rhs_scale=w2s[:, gg, :],
-                        start=(gg == 0),
-                        stop=(gg == G2 - 1),
-                    )
             for jt in range(2):
                 nc.scalar.activation(
                     out=zT_sb[:, jt, col0 : col0 + ncols], in_=zt[jt], func=AF.Identity, bias=b2T[:, jt : jt + 1], scale=1.0
                 )
-            for k, bank in enumerate(zb):
-                i = i0 + 2 * k
-                nc.vector.tensor_tensor(
-                    out=z_sb[:, i : i + 2, :],
-                    in0=bank[:].rearrange("p (i j) -> p i j", i=2),
-                    in1=b2bc[:].unsqueeze(1).to_broadcast([P, 2, H1]),
-                    op=ALU.add,
-                )
-            nc.sync.dma_start(out=z_view[:, i0 : i0 + nt, :], in_=z_sb[:, i0 : i0 + nt, :])
+
+        st = {}
+
+        def d_pe(col0, ncols, share=None):
+            i0, nt = col0 // P, ncols // P
+            zb = []
+            for ii in range(nt):
+                if ii % 2 == 0:
+                    zb.append(new_bank())
+                for jt in range(2):
+                    off = H1 * (ii % 2) + P * jt
+                    nc.tensor.transpose(zb[-1][:, off : off + P], zT_sb[:, jt, P * (i0 + ii) : P * (i0 + ii + 1)], ident_f[:])
+            db = new_bank() if share is None else st[share][1]
+            slot0 = 0 if share is None else i0 - share // P
+            for ii in range(nt):
+                i = i0 + ii
+                for jt in range(2):
+                    nc.tensor.matmul(
+                        out=db[:, 32 * (slot0 + ii) : 32 * (slot0 + ii) + NCL],
+                        lhsT=zT_sb[:, jt, P * i : P * (i + 1)],
+                        rhs=cTm2[:, jt, :],
+                        start=(jt == 0),
+                        stop=(jt == 1),
+                    )
+            st[col0] = (zb, db)
+
+        def d_sq(col0, ncols):
+            i0, nt = col0 // P, ncols // P
+            zb = st[col0][0]
             for ii in range(nt):
                 junk = small.tile([P, H1], F32, tag="junk", name="junk")
-                nc.scalar.activation(out=junk[:], in_=z_sb[:, i0 + ii, :], func=AF.Square, accum_out=z2[:, i0 + ii : i0 + ii + 1])
+                nc.scalar.activation(
+                    out=junk[:], in_=zb[ii // 2][:, H1 * (ii % 2) : H1 * (ii % 2 + 1)], func=AF.Square, accum_out=z2[:, i0 + ii : i0 + ii + 1]
+                )
 
-        def dist(col0, ncols):
+        def d_zc(col0, ncols, engine):
+            i0, nt = col0 // P, ncols // P
+            for k, bank in enumerate(st[col0][0]):
+                dst = z_sb[:, i0 + 2 * k : i0 + 2 * k + 2, :].rearrange("p i j -> p (i j)")
+                if engine == "s":
+                    nc.scalar.copy(out=dst, in_=bank[:])
+                else:
+                    nc.vector.tensor_copy(out=dst, in_=bank[:])
+            nc.sync.dma_start(out=z_view[:, i0 : i0 + nt, :], in_=z_sb[:, i0 : i0 + nt, :])
+
+        def d_v(col0, ncols):
             i0, nt = col0 // P, ncols // P
             shape = [P, nt, NCL]
+            db = st[col0][1]
             ee = small.tile(shape, F32, tag="ee%d" % nt, name="ee")
             nc.vector.tensor_tensor(
                 out=ee[:],
@@ -280,17 +292,6 @@ def tile_lintrans_pa_kernel(tc, x, W1, b1, W2, b2, clusters, out_0, out_1):
                 in1=z2[:, i0 : i0 + nt].unsqueeze(2).to_broadcast(shape),
                 op=ALU.add,
             )
-            db = new_bank()
-            for ii in range(nt):
-                i = i0 + ii
-                for jt in range(2):
-                    nc.tensor.matmul(
-                        out=db[:, 32 * ii : 32 * ii + NCL],
-                        lhsT=zT_sb[:, jt, P * i : P * (i + 1)],
-                        rhs=cTm2[:, jt, :],
-                        start=(jt == 0),
-                        stop=(jt == 1),
-                    )
             dview = db[:, 0 : 32 * nt].rearrange("p (i k) -> p i k", k=32)[:, :, 0:NCL]
             dd = small.tile(shape, F32, tag="dd%d" % nt, name="dd")
             nc.vector.tensor_tensor(out=dd[:], in0=dview, in1=ee[:], op=ALU.add)
@@ -322,7 +323,7 @@ def tile_lintrans_pa_kernel(tc, x, W1, b1, W2, b2, clusters, out_0, out_1):
         units = [(i, gp) for i in range(8) for gp in range(3)]
         for n, (i, gp) in enumerate(units):
             x_transpose(i, gp)
-            if n >= 2:
+            if 2 <= n < 23:
                 x_quantise(*units[n - 2])
             if gp == 2:
                 if i + XR_BUFS < 8:
@@ -335,17 +336,17 @@ def tile_lintrans_pa_kernel(tc, x, W1, b1, W2, b2, clusters, out_0, out_1):
                         load_w(0, c)
                 if i == 1:
                     small_prep()
+                if i == 3:
+                    small_prep3(small_prep2())
                 if i == 6:
                     w_rg(0, 0)
-            if (i, gp) == (7, 1):
+            if (i, gp) == (7, 0):
                 w_q(0, 0)
-        x_quantise(*units[-2])
-        x_quantise(*units[-1])
-        small_prep2()
+        x_quantise(7, 0)
 
         acc = {}
-        for m in range(4):
-            for b in range(2):
+        for b in range(2):
+            for m in range(4):
                 acc[(m, b)] = new_bank()
         w_rg(0, 1)
         for c in range(G1):
@@ -354,22 +355,22 @@ def tile_lintrans_pa_kernel(tc, x, W1, b1, W2, b2, clusters, out_0, out_1):
             if c > 0:
                 w_q(0, c)
             load_w(1, c)
-            for m in range(4):
-                for b in range(2):
+            if c in (1, 3):
+                x_quantise(7, (c + 1) // 2)
+            for b in range(2):
+                for m in range(4):
                     l1_pass(acc[(m, b)], m, c, 512 * b, 512)
         load_w2()
         for c in range(4):
             w_rg(1, c)
             w_q(1, c)
-        for m in range(2):
-            for b in range(2):
-                silu(acc[(m, b)], m, 512 * b, 512)
+        for m in range(4):
+            silu(acc[(m, 0)], m, 0, 512)
         for c in range(4, G1):
             w_rg(1, c)
             w_q(1, c)
-        for m in range(2, 4):
-            for b in range(2):
-                silu(acc[(m, b)], m, 512 * b, 512)
+        for m in range(4):
+            silu(acc[(m, 1)], m, 512, 512)
         acca = {}
         for m in range(4, 8):
             acca[m] = new_bank()
@@ -398,7 +399,15 @@ def tile_lintrans_pa_kernel(tc, x, W1, b1, W2, b2, clusters, out_0, out_1):
         layer2(0, 512)
         round2(768, 256, range(6, 8))
         layer2(512, 256)
-        dist(0, 512)
+        d_pe(0, 512)
+        d_sq(0, 512)
         layer2(768, 256)
-        dist(512, 256)
-        dist(768, 256)
+        d_zc(0, 512, "v")
+        d_v(0, 512)
+        d_pe(512, 256)
+        d_sq(512, 256)
+        d_pe(768, 256, share=512)
+        d_sq(768, 256)
+        d_zc(512, 256, "v")
+        d_zc(768, 256, "s")
+        d_v(512, 512)

@@ -25,6 +25,9 @@ XR_BUFS = 5
 EARLY_AFTER = 6
 N_EARLY = 1
 WR_BUFS = 6
+WARM0 = 8
+WARM1 = 2
+WARM2 = 5
 
 
 def tile_lintrans_pa_kernel(tc, x, W1, b1, W2, b2, clusters, out_0, out_1):
@@ -49,6 +52,11 @@ def tile_lintrans_pa_kernel(tc, x, W1, b1, W2, b2, clusters, out_0, out_1):
             bank_no[0] += 1
             return psum.tile([P, cols], dtype, tag="bank%d" % k, name="bank%d" % k)
 
+        def keep_clock(n):
+            bank = new_bank()
+            for r in range(n):
+                nc.tensor.matmul(out=bank[:], lhsT=dz[:, 0:P], rhs=dz[:], start=True, stop=True)
+
         x_view = x.rearrange("(p i) k -> p i k", i=8)
         z_view = out_0.rearrange("(p i) j -> p i j", i=8)
         q_view = out_1.rearrange("(p i) k -> p i k", i=8)
@@ -61,6 +69,8 @@ def tile_lintrans_pa_kernel(tc, x, W1, b1, W2, b2, clusters, out_0, out_1):
         nc.vector.memset(misc[:], 0.0)
         ones_f = const.tile([P, P], F32, name="ones_f")
         nc.vector.memset(ones_f[:], 1.0)
+        dz = const.tile([P, 512], BF16, name="dz")
+        nc.vector.memset(dz[:], 0.0)
         warm = const.tile([P, 2], F32, name="warm")
         nc.vector.memset(warm[:], 0.0)
         nc.scalar.dma_start(out=misc[0:NCL, :], in_=clusters)
@@ -274,11 +284,12 @@ def tile_lintrans_pa_kernel(tc, x, W1, b1, W2, b2, clusters, out_0, out_1):
         def d_zc(col0, ncols, engine):
             i0, nt = col0 // P, ncols // P
             for k, bank in enumerate(st[col0][0]):
-                dst = z_sb[:, i0 + 2 * k : i0 + 2 * k + 2, :].rearrange("p i j -> p (i j)")
+                n_in = min(2, nt - 2 * k)
+                dst = z_sb[:, i0 + 2 * k : i0 + 2 * k + n_in, :].rearrange("p i j -> p (i j)")
                 if engine == "s":
-                    nc.scalar.copy(out=dst, in_=bank[:])
+                    nc.scalar.copy(out=dst, in_=bank[:, 0 : H1 * n_in])
                 else:
-                    nc.vector.tensor_copy(out=dst, in_=bank[:])
+                    nc.vector.tensor_copy(out=dst, in_=bank[:, 0 : H1 * n_in])
             nc.sync.dma_start(out=z_view[:, i0 : i0 + nt, :], in_=z_sb[:, i0 : i0 + nt, :])
 
         def d_v(col0, ncols):
@@ -320,12 +331,15 @@ def tile_lintrans_pa_kernel(tc, x, W1, b1, W2, b2, clusters, out_0, out_1):
 
         for i in range(XR_BUFS):
             load_x(i)
+        keep_clock(WARM0)
         units = [(i, gp) for i in range(8) for gp in range(3)]
         for n, (i, gp) in enumerate(units):
             x_transpose(i, gp)
             if 2 <= n < 23:
                 x_quantise(*units[n - 2])
             if gp == 2:
+                if i < 7:
+                    keep_clock(WARM1 if i < 6 else WARM2)
                 if i + XR_BUFS < 8:
                     load_x(i + XR_BUFS)
                 if i + XR_BUFS == EARLY_AFTER:

@@ -28,6 +28,7 @@ WR_BUFS = 6
 WARM0 = 8
 WARM1 = 2
 WARM2 = 5
+X_PIECES = {7: 3}
 
 
 def tile_lintrans_pa_kernel(tc, x, W1, b1, W2, b2, clusters, out_0, out_1):
@@ -41,7 +42,7 @@ def tile_lintrans_pa_kernel(tc, x, W1, b1, W2, b2, clusters, out_0, out_1):
         wraw = ctx.enter_context(tc.tile_pool(name="wraw", bufs=WR_BUFS))
         xgp = ctx.enter_context(tc.tile_pool(name="xgp", bufs=6))
         wgp = ctx.enter_context(tc.tile_pool(name="wgp", bufs=3))
-        hgp = ctx.enter_context(tc.tile_pool(name="hgp", bufs=2))
+        hgp = ctx.enter_context(tc.tile_pool(name="hgp", bufs=4))
         small = ctx.enter_context(tc.tile_pool(name="small", bufs=2))
         psum = ctx.enter_context(tc.psum_pool(name="psum", bufs=1))
 
@@ -104,7 +105,10 @@ def tile_lintrans_pa_kernel(tc, x, W1, b1, W2, b2, clusters, out_0, out_1):
 
         def load_x(i):
             xr[i] = xraw.tile([P, D_IN], BF16, tag="xr", name="xr")
-            nc.sync.dma_start(out=xr[i][:], in_=x_view[:, i, :])
+            pieces = X_PIECES.get(i, 1)
+            step = D_IN // pieces
+            for s in range(pieces):
+                nc.sync.dma_start(out=xr[i][:, step * s : step * (s + 1)], in_=x_view[:, i, step * s : step * (s + 1)])
 
         def load_w(side, c):
             wr[(side, c)] = wraw.tile([P, 4, 512], BF16, tag="wr", name="wr")
@@ -204,20 +208,22 @@ def tile_lintrans_pa_kernel(tc, x, W1, b1, W2, b2, clusters, out_0, out_1):
             )
 
         def h_quantise(col0, ncols, gg):
-            hg = hgp.tile([P, ncols, 4], BF16, tag="hg", name="hg", align_bytes=64)
-            regroup("v", hg[:], h_bf[:, 4 * gg : 4 * (gg + 1), col0 : col0 + ncols])
-            return hg
+            hg = hgp.tile([P, 512, 4], BF16, tag="hg", name="hg", align_bytes=64)
+            regroup("v", hg[:, 0:ncols, :], h_bf[:, 4 * gg : 4 * (gg + 1), col0 : col0 + ncols])
+            return hg[:, 0:ncols, :]
 
         def h_quantise2(hg, col0, ncols, gg):
             nc.vector.quantize_mx(
                 out=hq[:, gg, col0 : col0 + ncols].bitcast(FP8X4),
                 scales=hs[:, gg, col0 : col0 + ncols],
-                in_=hg[:].rearrange("p n t -> p (n t)"),
+                in_=hg.rearrange("p n t -> p (n t)"),
             )
 
-        def w2_prep():
+        def w2_regroup():
             for gg in range(G2):
                 regroup("v", w2g[:, gg, :, :], w2r[:, 4 * gg : 4 * (gg + 1), :])
+
+        def w2_quantise():
             nc.vector.quantize_mx(
                 out=w2q[:].rearrange("p g j -> p (g j)").bitcast(FP8X4),
                 scales=w2s[:].rearrange("p g j -> p (g j)"),
@@ -292,30 +298,40 @@ def tile_lintrans_pa_kernel(tc, x, W1, b1, W2, b2, clusters, out_0, out_1):
                     nc.vector.tensor_copy(out=dst, in_=bank[:, 0 : H1 * n_in])
             nc.sync.dma_start(out=z_view[:, i0 : i0 + nt, :], in_=z_sb[:, i0 : i0 + nt, :])
 
-        def d_v(col0, ncols):
-            i0, nt = col0 // P, ncols // P
-            shape = [P, nt, NCL]
-            db = st[col0][1]
-            ee = small.tile(shape, F32, tag="ee%d" % nt, name="ee")
-            nc.vector.tensor_tensor(
-                out=ee[:],
-                in0=cc1[:].unsqueeze(1).to_broadcast(shape),
-                in1=z2[:, i0 : i0 + nt].unsqueeze(2).to_broadcast(shape),
-                op=ALU.add,
-            )
-            dview = db[:, 0 : 32 * nt].rearrange("p (i k) -> p i k", k=32)[:, :, 0:NCL]
-            dd = small.tile(shape, F32, tag="dd%d" % nt, name="dd")
-            nc.vector.tensor_tensor(out=dd[:], in0=dview, in1=ee[:], op=ALU.add)
-            tt = small.tile(shape, F32, tag="tt%d" % nt, name="tt")
-            nc.vector.reciprocal(out=tt[:], in_=dd[:])
-            sm = small.tile([P, nt], F32, tag="sm%d" % nt, name="sm")
-            nc.vector.reduce_sum(out=sm[:], in_=tt[:], axis=AX.X)
-            rs = small.tile([P, nt], F32, tag="rs%d" % nt, name="rs")
-            nc.vector.reciprocal(out=rs[:], in_=sm[:])
-            nc.vector.tensor_tensor(
-                out=q_sb[:, i0 : i0 + nt, :], in0=tt[:], in1=rs[:].unsqueeze(2).to_broadcast(shape), op=ALU.mult
-            )
-            nc.sync.dma_start(out=q_view[:, i0 : i0 + nt, :], in_=q_sb[:, i0 : i0 + nt, :])
+        def d_v(parts):
+            work = []
+            for i0, nt, db, slot0 in parts:
+                shape = [P, nt, NCL]
+                names = ["%s%d_%d" % (s, nt, i0 % 4) for s in ("ee", "dd", "tt", "sm", "rs")]
+                ee = small.tile(shape, F32, tag=names[0], name=names[0])
+                dd = small.tile(shape, F32, tag=names[1], name=names[1])
+                tt = small.tile(shape, F32, tag=names[2], name=names[2])
+                sm = small.tile([P, nt], F32, tag=names[3], name=names[3])
+                rs = small.tile([P, nt], F32, tag=names[4], name=names[4])
+                dview = db[:, 32 * slot0 : 32 * (slot0 + nt)].rearrange("p (i k) -> p i k", k=32)[:, :, 0:NCL]
+                work.append((i0, nt, shape, dview, ee, dd, tt, sm, rs))
+            for i0, nt, shape, dview, ee, dd, tt, sm, rs in work:
+                nc.vector.tensor_tensor(
+                    out=ee[:],
+                    in0=cc1[:].unsqueeze(1).to_broadcast(shape),
+                    in1=z2[:, i0 : i0 + nt].unsqueeze(2).to_broadcast(shape),
+                    op=ALU.add,
+                )
+            for i0, nt, shape, dview, ee, dd, tt, sm, rs in work:
+                nc.vector.tensor_tensor(out=dd[:], in0=dview, in1=ee[:], op=ALU.add)
+            for i0, nt, shape, dview, ee, dd, tt, sm, rs in work:
+                nc.vector.reciprocal(out=tt[:], in_=dd[:])
+            for i0, nt, shape, dview, ee, dd, tt, sm, rs in work:
+                nc.vector.reduce_sum(out=sm[:], in_=tt[:], axis=AX.X)
+            for i0, nt, shape, dview, ee, dd, tt, sm, rs in work:
+                nc.vector.reciprocal(out=rs[:], in_=sm[:])
+            for i0, nt, shape, dview, ee, dd, tt, sm, rs in work:
+                nc.vector.tensor_tensor(
+                    out=q_sb[:, i0 : i0 + nt, :], in0=tt[:], in1=rs[:].unsqueeze(2).to_broadcast(shape), op=ALU.mult
+                )
+            first = parts[0][0]
+            last = parts[-1][0] + parts[-1][1]
+            nc.sync.dma_start(out=q_view[:, first:last, :], in_=q_sb[:, first:last, :])
 
         def w_rg(side, c):
             w_regroup(side, c, 0, "v")
@@ -362,26 +378,29 @@ def tile_lintrans_pa_kernel(tc, x, W1, b1, W2, b2, clusters, out_0, out_1):
         for b in range(2):
             for m in range(4):
                 acc[(m, b)] = new_bank()
+        halves = [(side, c) for side in range(2) for c in range(G1)]
         w_rg(0, 1)
+        x_quantise(7, 1)
         for c in range(G1):
-            if 0 < c < G1 - 1:
-                w_rg(0, c + 1)
             if c > 0:
+                w_rg(*halves[c + 1])
                 w_q(0, c)
+            if c == 1:
+                x_quantise(7, 2)
             load_w(1, c)
-            if c in (1, 3):
-                x_quantise(7, (c + 1) // 2)
-            for b in range(2):
-                for m in range(4):
-                    l1_pass(acc[(m, b)], m, c, 512 * b, 512)
+            if c in (0, G1 - 1):
+                order = [(m, b) for b in range(2) for m in range(4)]
+            else:
+                order = [(m, b) for m in range(4) for b in range(2)]
+            for m, b in order:
+                l1_pass(acc[(m, b)], m, c, 512 * b, 512)
         load_w2()
-        for c in range(4):
-            w_rg(1, c)
-            w_q(1, c)
-        for m in range(4):
-            silu(acc[(m, 0)], m, 0, 512)
-        for c in range(4, G1):
-            w_rg(1, c)
+        for c in range(G1):
+            if c == 3:
+                for m in range(4):
+                    silu(acc[(m, 0)], m, 0, 512)
+            if c + 1 < G1:
+                w_rg(1, c + 1)
             w_q(1, c)
         for m in range(4):
             silu(acc[(m, 1)], m, 512, 512)
@@ -391,13 +410,18 @@ def tile_lintrans_pa_kernel(tc, x, W1, b1, W2, b2, clusters, out_0, out_1):
         for g in range(G1):
             for m in range(4, 8):
                 l1_pass(acca[m], m, g, 0, 512)
-        w2_prep()
-        hq_all(0, 512, 0)
-        hq_all(512, 256, 0)
-        hq_all(768, 256, 0)
+        w2_regroup()
+        hga0 = h_quantise(0, 512, 0)
+        w2_quantise()
+        hgb0 = h_quantise(512, 256, 0)
+        h_quantise2(hga0, 0, 512, 0)
+        hgc0 = h_quantise(768, 256, 0)
+        h_quantise2(hgb0, 512, 256, 0)
         for m in range(4, 8):
             silu(acca[m], m, 0, 512)
-        hq_all(0, 512, 1)
+        hga1 = h_quantise(0, 512, 1)
+        h_quantise2(hgc0, 768, 256, 0)
+        h_quantise2(hga1, 0, 512, 1)
 
         def round2(col0, ncols, ms):
             for m in ms:
@@ -417,11 +441,11 @@ def tile_lintrans_pa_kernel(tc, x, W1, b1, W2, b2, clusters, out_0, out_1):
         d_sq(0, 512)
         layer2(768, 256)
         d_zc(0, 512, "v")
-        d_v(0, 512)
+        d_v([(0, 2, st[0][1], 0), (2, 2, st[0][1], 2)])
         d_pe(512, 256)
         d_sq(512, 256)
         d_pe(768, 256, share=512)
         d_sq(768, 256)
         d_zc(512, 256, "v")
         d_zc(768, 256, "s")
-        d_v(512, 512)
+        d_v([(4, 2, st[512][1], 0), (6, 2, st[512][1], 2)])

@@ -79,17 +79,17 @@ def tile_lintrans_pa_kernel(tc, x, W1, b1, W2, b2, clusters, out_0, out_1):
         nc.scalar.dma_start(out=misc[64:66, 0:P], in_=b2.rearrange("(a p) -> a p", p=P))
         nc.scalar.activation(out=warm[:, 1:2], in_=warm[:, 0:1], func=AF.Silu)
 
-        xq = keep.tile([P, G1, N_ROWS], U32, name="xq", align_bytes=64)
-        xs = keep.tile([P, G1, N_ROWS], U8, name="xs", align_bytes=64)
-        wq = keep.tile([P, G1, H0], U32, name="wq", align_bytes=64)
-        ws = keep.tile([P, G1, H0], U8, name="ws", align_bytes=64)
+        xq = keep.tile([P, G1, N_ROWS], U32, name="xq", align_bytes=256)
+        xs = keep.tile([P, G1, N_ROWS], U8, name="xs", align_bytes=256)
+        wq = keep.tile([P, G1, H0], U32, name="wq", align_bytes=256)
+        ws = keep.tile([P, G1, H0], U8, name="ws", align_bytes=256)
         h_bf = keep.tile([P, MT, N_ROWS], BF16, name="h_bf")
-        hq = keep.tile([P, G2, N_ROWS], U32, name="hq", align_bytes=64)
-        hs = keep.tile([P, G2, N_ROWS], U8, name="hs", align_bytes=64)
+        hq = keep.tile([P, G2, N_ROWS], U32, name="hq", align_bytes=256)
+        hs = keep.tile([P, G2, N_ROWS], U8, name="hs", align_bytes=256)
         w2r = keep.tile([P, G2 * 4, H1], BF16, name="w2r")
-        w2g = keep.tile([P, G2, H1, 4], BF16, name="w2g", align_bytes=64)
-        w2q = keep.tile([P, G2, H1], U32, name="w2q", align_bytes=64)
-        w2s = keep.tile([P, G2, H1], U8, name="w2s", align_bytes=64)
+        w2g = keep.tile([P, G2, H1, 4], BF16, name="w2g", align_bytes=256)
+        w2q = keep.tile([P, G2, H1], U32, name="w2q", align_bytes=256)
+        w2s = keep.tile([P, G2, H1], U8, name="w2s", align_bytes=256)
         zT_sb = keep.tile([P, 2, N_ROWS], F32, name="zT_sb")
         z_sb = keep.tile([P, 8, H1], F32, name="z_sb")
         q_sb = keep.tile([P, 8, NCL], F32, name="q_sb")
@@ -130,7 +130,7 @@ def tile_lintrans_pa_kernel(tc, x, W1, b1, W2, b2, clusters, out_0, out_1):
             words = xr[i][:].bitcast(F32)
             for s in range(4):
                 nc.tensor.transpose(bank[:, P * s : P * (s + 1)], words[:, 512 * gp + P * s : 512 * gp + P * (s + 1)], ident_f[:])
-            xg[u] = xgp.tile([P, 1024], BF16, tag="xg", name="xg", align_bytes=64)
+            xg[u] = xgp.tile([P, 1024], BF16, tag="xg", name="xg", align_bytes=256)
             dst = xg[u][:].bitcast(F32).rearrange("p (g n u) -> p g n u", g=2, u=2)
             src = bank[:].rearrange("p (g u n) -> p g n u", g=2, u=2)
             if u in CO_ON_VECTOR:
@@ -178,7 +178,7 @@ def tile_lintrans_pa_kernel(tc, x, W1, b1, W2, b2, clusters, out_0, out_1):
 
         def w_regroup(side, c, quarter, engine):
             if (side, c) not in wg:
-                wg[(side, c)] = wgp.tile([P, 512, 4], BF16, tag="wg", name="wg", align_bytes=64)
+                wg[(side, c)] = wgp.tile([P, 512, 4], BF16, tag="wg", name="wg", align_bytes=256)
             cols = slice(256 * quarter, 256 * (quarter + 1))
             regroup(engine, wg[(side, c)][:, cols, :], wr[(side, c)][:, :, cols])
 
@@ -208,7 +208,7 @@ def tile_lintrans_pa_kernel(tc, x, W1, b1, W2, b2, clusters, out_0, out_1):
             )
 
         def h_quantise(col0, ncols, gg):
-            hg = hgp.tile([P, 512, 4], BF16, tag="hg", name="hg", align_bytes=64)
+            hg = hgp.tile([P, 512, 4], BF16, tag="hg", name="hg", align_bytes=256)
             regroup("v", hg[:, 0:ncols, :], h_bf[:, 4 * gg : 4 * (gg + 1), col0 : col0 + ncols])
             return hg[:, 0:ncols, :]
 
@@ -302,30 +302,30 @@ def tile_lintrans_pa_kernel(tc, x, W1, b1, W2, b2, clusters, out_0, out_1):
             work = []
             for i0, nt, db, slot0 in parts:
                 shape = [P, nt, NCL]
-                names = ["%s%d_%d" % (s, nt, i0 % 4) for s in ("ee", "dd", "tt", "sm", "rs")]
-                ee = small.tile(shape, F32, tag=names[0], name=names[0])
-                dd = small.tile(shape, F32, tag=names[1], name=names[1])
-                tt = small.tile(shape, F32, tag=names[2], name=names[2])
-                sm = small.tile([P, nt], F32, tag=names[3], name=names[3])
-                rs = small.tile([P, nt], F32, tag=names[4], name=names[4])
+                names = ["%s%d_%d" % (s, nt, i0 % 4) for s in ("dd", "tt", "sm", "rs")]
+                dd = small.tile(shape, F32, tag=names[0], name=names[0])
+                tt = small.tile(shape, F32, tag=names[1], name=names[1])
+                sm = small.tile([P, nt], F32, tag=names[2], name=names[2])
+                rs = small.tile([P, nt], F32, tag=names[3], name=names[3])
                 dview = db[:, 32 * slot0 : 32 * (slot0 + nt)].rearrange("p (i k) -> p i k", k=32)[:, :, 0:NCL]
-                work.append((i0, nt, shape, dview, ee, dd, tt, sm, rs))
-            for i0, nt, shape, dview, ee, dd, tt, sm, rs in work:
-                nc.vector.tensor_tensor(
-                    out=ee[:],
-                    in0=cc1[:].unsqueeze(1).to_broadcast(shape),
-                    in1=z2[:, i0 : i0 + nt].unsqueeze(2).to_broadcast(shape),
-                    op=ALU.add,
-                )
-            for i0, nt, shape, dview, ee, dd, tt, sm, rs in work:
-                nc.vector.tensor_tensor(out=dd[:], in0=dview, in1=ee[:], op=ALU.add)
-            for i0, nt, shape, dview, ee, dd, tt, sm, rs in work:
+                work.append((i0, nt, shape, dview, dd, tt, sm, rs))
+            for i0, nt, shape, dview, dd, tt, sm, rs in work:
+                for ii in range(nt):
+                    nc.vector.scalar_tensor_tensor(
+                        out=dd[:, ii, :],
+                        in0=dview[:, ii, :],
+                        scalar=z2[:, i0 + ii : i0 + ii + 1],
+                        in1=cc1[:],
+                        op0=ALU.add,
+                        op1=ALU.add,
+                    )
+            for i0, nt, shape, dview, dd, tt, sm, rs in work:
                 nc.vector.reciprocal(out=tt[:], in_=dd[:])
-            for i0, nt, shape, dview, ee, dd, tt, sm, rs in work:
+            for i0, nt, shape, dview, dd, tt, sm, rs in work:
                 nc.vector.reduce_sum(out=sm[:], in_=tt[:], axis=AX.X)
-            for i0, nt, shape, dview, ee, dd, tt, sm, rs in work:
+            for i0, nt, shape, dview, dd, tt, sm, rs in work:
                 nc.vector.reciprocal(out=rs[:], in_=sm[:])
-            for i0, nt, shape, dview, ee, dd, tt, sm, rs in work:
+            for i0, nt, shape, dview, dd, tt, sm, rs in work:
                 nc.vector.tensor_tensor(
                     out=q_sb[:, i0 : i0 + nt, :], in0=tt[:], in1=rs[:].unsqueeze(2).to_broadcast(shape), op=ALU.mult
                 )

@@ -20,7 +20,7 @@ MT = H0 // P
 FLOPS = 2 * N_ROWS * D_IN * H0 + 2 * N_ROWS * H0 * H1 + 3 * N_ROWS * H1 * NCL
 
 PIN = True
-CO_ON_VECTOR = (4, 9, 14, 19, 22)
+CO_ON_VECTOR = (4, 9, 14, 17, 20, 22)
 XR_BUFS = 5
 EARLY_AFTER = 6
 N_EARLY = 1
@@ -302,7 +302,7 @@ def tile_lintrans_pa_kernel(tc, x, W1, b1, W2, b2, clusters, out_0, out_1):
             work = []
             for i0, nt, db, slot0 in parts:
                 shape = [P, nt, NCL]
-                names = ["%s%d_%d" % (s, nt, i0 % 4) for s in ("dd", "tt", "sm", "rs")]
+                names = ["%s%d_%d" % (s, nt, i0) for s in ("dd", "tt", "sm", "rs")]
                 dd = small.tile(shape, F32, tag=names[0], name=names[0])
                 tt = small.tile(shape, F32, tag=names[1], name=names[1])
                 sm = small.tile([P, nt], F32, tag=names[2], name=names[2])
@@ -382,10 +382,13 @@ def tile_lintrans_pa_kernel(tc, x, W1, b1, W2, b2, clusters, out_0, out_1):
         w_rg(0, 1)
         x_quantise(7, 1)
         for c in range(G1):
-            if c > 0:
+            if c == 1:
+                w_q(0, c)
+                w_rg(*halves[c + 1])
+            elif c > 1:
                 w_rg(*halves[c + 1])
                 w_q(0, c)
-            if c == 1:
+            if c == 2:
                 x_quantise(7, 2)
             load_w(1, c)
             if c in (0, G1 - 1):
@@ -423,29 +426,38 @@ def tile_lintrans_pa_kernel(tc, x, W1, b1, W2, b2, clusters, out_0, out_1):
         h_quantise2(hgc0, 768, 256, 0)
         h_quantise2(hga1, 0, 512, 1)
 
-        def round2(col0, ncols, ms):
+        def round2(col0, ncols, ms, split=False):
             for m in ms:
                 a = new_bank()
                 for g in range(G1):
                     l1_pass(a, m, g, col0, ncols)
                 silu(a, m, col0, ncols)
-                if m == 7:
+                if m == 7 and not split:
                     hq_all(col0, ncols, 1)
+                if m == 7 and split:
+                    ha = h_quantise(col0, 128, 1)
+                    hb = h_quantise(col0 + 128, 128, 1)
+                    h_quantise2(ha, col0, 128, 1)
+                    h_quantise2(hb, col0 + 128, 128, 1)
 
         round2(512, 256, range(4, 8))
         round2(768, 256, range(4, 6))
         layer2(0, 512)
-        round2(768, 256, range(6, 8))
+        round2(768, 256, range(6, 8), split=True)
         layer2(512, 256)
         d_pe(0, 512)
         d_sq(0, 512)
-        layer2(768, 256)
+        layer2(768, 128)
+        layer2(896, 128)
         d_zc(0, 512, "v")
         d_v([(0, 2, st[0][1], 0), (2, 2, st[0][1], 2)])
         d_pe(512, 256)
         d_sq(512, 256)
-        d_pe(768, 256, share=512)
-        d_sq(768, 256)
+        d_pe(768, 128, share=512)
+        d_pe(896, 128, share=512)
+        d_sq(768, 128)
+        d_sq(896, 128)
         d_zc(512, 256, "v")
-        d_zc(768, 256, "s")
+        d_zc(768, 128, "s")
+        d_zc(896, 128, "s")
         d_v([(4, 2, st[512][1], 0), (6, 2, st[512][1], 2)])

@@ -169,8 +169,8 @@ def tile_lintrans_pa_kernel(tc, x, W1, b1, W2, b2, clusters, out_0, out_1):
         wg = {}
 
         def regroup(engine, dst, src):
-            d = dst.rearrange("p (c i) t -> p c t i", i=4)
-            s = src.rearrange("p t (c i) -> p c t i", i=4)
+            d = dst.rearrange("p (c i) t -> p c t i", i=8)
+            s = src.rearrange("p t (c i) -> p c t i", i=8)
             if engine == "v":
                 nc.vector.tensor_copy(out=d, in_=s)
             else:

@@ -219,9 +219,8 @@ def tile_lintrans_pa_kernel(tc, x, W1, b1, W2, b2, clusters, out_0, out_1):
                 in_=hg.rearrange("p n t -> p (n t)"),
             )
 
-        def w2_regroup():
-            for gg in range(G2):
-                regroup("v", w2g[:, gg, :, :], w2r[:, 4 * gg : 4 * (gg + 1), :])
+        def w2_regroup(gg):
+            regroup("v", w2g[:, gg, :, :], w2r[:, 4 * gg : 4 * (gg + 1), :])
 
         def w2_quantise():
             nc.vector.quantize_mx(
@@ -405,6 +404,10 @@ def tile_lintrans_pa_kernel(tc, x, W1, b1, W2, b2, clusters, out_0, out_1):
             if c + 1 < G1:
                 w_rg(1, c + 1)
             w_q(1, c)
+            if c == 4:
+                w2_regroup(0)
+            if c == 5:
+                w2_regroup(1)
         for m in range(4):
             silu(acc[(m, 1)], m, 512, 512)
         acca = {}
@@ -413,7 +416,6 @@ def tile_lintrans_pa_kernel(tc, x, W1, b1, W2, b2, clusters, out_0, out_1):
         for g in range(G1):
             for m in range(4, 8):
                 l1_pass(acca[m], m, g, 0, 512)
-        w2_regroup()
         hga0 = h_quantise(0, 512, 0)
         w2_quantise()
         hgb0 = h_quantise(512, 256, 0)
@@ -441,9 +443,9 @@ def tile_lintrans_pa_kernel(tc, x, W1, b1, W2, b2, clusters, out_0, out_1):
                     h_quantise2(hb, col0 + 128, 128, 1)
 
         round2(512, 256, range(4, 8))
-        round2(768, 256, range(4, 6))
+        round2(768, 256, range(4, 7))
         layer2(0, 512)
-        round2(768, 256, range(6, 8), split=True)
+        round2(768, 256, range(7, 8), split=True)
         layer2(512, 256)
         d_pe(0, 512)
         d_sq(0, 512)

@@ -398,7 +398,7 @@ def tile_lintrans_pa_kernel(tc, x, W1, b1, W2, b2, clusters, out_0, out_1):
                 l1_pass(acc[(m, b)], m, c, 512 * b, 512)
         load_w2()
         for c in range(G1):
-            if c == 3:
+            if c == 2:
                 for m in range(4):
                     silu(acc[(m, 0)], m, 0, 512)
             if c + 1 < G1:

from contextlib import ExitStack

import concourse.mybir as mybir
from concourse.masks import make_identity

F32 = mybir.dt.float32
BF16 = mybir.dt.bfloat16
U32 = mybir.dt.uint32
U8 = mybir.dt.uint8
FP8X4 = mybir.dt.float8_e4m3fn_x4
AF = mybir.ActivationFunctionType
ALU = mybir.AluOpType
AX = mybir.AxisListType

P = 128
N_ROWS, D_IN, H0, H1, NCL = 1024, 3072, 1024, 256, 20
G1 = D_IN // 512
G2 = H0 // 512
MT = H0 // P
FLOPS = 2 * N_ROWS * D_IN * H0 + 2 * N_ROWS * H0 * H1 + 3 * N_ROWS * H1 * NCL

PIN = True
CO_ON_VECTOR = (4, 9, 14, 17, 20, 22)
XR_BUFS = 5
EARLY_AFTER = 6
N_EARLY = 1
WR_BUFS = 6
WARM0 = 8
WARM1 = 2
WARM2 = 5
X_PIECES = {7: 3}


def tile_lintrans_pa_kernel(tc, x, W1, b1, W2, b2, clusters, out_0, out_1):
    nc = tc.nc
    with ExitStack() as ctx:
        if PIN:
            ctx.enter_context(tc.manual_schedule())
        const = ctx.enter_context(tc.tile_pool(name="const", bufs=1))
        keep = ctx.enter_context(tc.tile_pool(name="keep", bufs=1))
        xraw = ctx.enter_context(tc.tile_pool(name="xraw", bufs=XR_BUFS))
        wraw = ctx.enter_context(tc.tile_pool(name="wraw", bufs=WR_BUFS))
        xgp = ctx.enter_context(tc.tile_pool(name="xgp", bufs=6))
        wgp = ctx.enter_context(tc.tile_pool(name="wgp", bufs=3))
        hgp = ctx.enter_context(tc.tile_pool(name="hgp", bufs=4))
        small = ctx.enter_context(tc.tile_pool(name="small", bufs=2))
        psum = ctx.enter_context(tc.psum_pool(name="psum", bufs=1))

        bank_no = [0]

        def new_bank(dtype=F32, cols=512):
            k = bank_no[0] % 8
            bank_no[0] += 1
            return psum.tile([P, cols], dtype, tag="bank%d" % k, name="bank%d" % k)

        def keep_clock(n):
            bank = new_bank()
            for r in range(n):
                nc.tensor.matmul(out=bank[:], lhsT=dz[:, 0:P], rhs=dz[:], start=True, stop=True)

        x_view = x.rearrange("(p i) k -> p i k", i=8)
        z_view = out_0.rearrange("(p i) j -> p i j", i=8)
        q_view = out_1.rearrange("(p i) k -> p i k", i=8)

        ident_f = const.tile([P, P], F32, name="ident_f")
        make_identity(nc, ident_f[:])
        ident_b = const.tile([P, P], BF16, name="ident_b")
        make_identity(nc, ident_b[:])
        misc = const.tile([P, 2 * P], BF16, name="misc")
        nc.vector.memset(misc[:], 0.0)
        ones_f = const.tile([P, P], F32, name="ones_f")
        nc.vector.memset(ones_f[:], 1.0)
        dz = const.tile([P, 512], BF16, name="dz")
        nc.vector.memset(dz[:], 0.0)
        warm = const.tile([P, 2], F32, name="warm")
        nc.vector.memset(warm[:], 0.0)
        nc.scalar.dma_start(out=misc[0:NCL, :], in_=clusters)
        nc.scalar.dma_start(out=misc[32 : 32 + MT, 0:P], in_=b1.rearrange("(m p) -> m p", p=P))
        nc.scalar.dma_start(out=misc[64:66, 0:P], in_=b2.rearrange("(a p) -> a p", p=P))
        nc.scalar.activation(out=warm[:, 1:2], in_=warm[:, 0:1], func=AF.Silu)

        xq = keep.tile([P, G1, N_ROWS], U32, name="xq", align_bytes=256)
        xs = keep.tile([P, G1, N_ROWS], U8, name="xs", align_bytes=256)
        wq = keep.tile([P, G1, H0], U32, name="wq", align_bytes=256)
        ws = keep.tile([P, G1, H0], U8, name="ws", align_bytes=256)
        h_bf = keep.tile([P, MT, N_ROWS], BF16, name="h_bf")
        hq = keep.tile([P, G2, N_ROWS], U32, name="hq", align_bytes=256)
        hs = keep.tile([P, G2, N_ROWS], U8, name="hs", align_bytes=256)
        w2r = keep.tile([P, G2 * 4, H1], BF16, name="w2r")
        w2g = keep.tile([P, G2, H1, 4], BF16, name="w2g", align_bytes=256)
        w2q = keep.tile([P, G2, H1], U32, name="w2q", align_bytes=256)
        w2s = keep.tile([P, G2, H1], U8, name="w2s", align_bytes=256)
        zT_sb = keep.tile([P, 2, N_ROWS], F32, name="zT_sb")
        z_sb = keep.tile([P, 8, H1], F32, name="z_sb")
        q_sb = keep.tile([P, 8, NCL], F32, name="q_sb")
        z2 = keep.tile([P, 8], F32, name="z2")
        b1T = keep.tile([P, MT], F32, name="b1T")
        b2T = keep.tile([P, 2], F32, name="b2T")
        cTm2 = keep.tile([P, 2, NCL], F32, name="cTm2")
        csq = keep.tile([P, 2, NCL], F32, name="csq")
        cc1 = keep.tile([P, NCL], F32, name="cc1")

        xr = {}
        wr = {}

        def load_x(i):
            xr[i] = xraw.tile([P, D_IN], BF16, tag="xr", name="xr")
            pieces = X_PIECES.get(i, 1)
            step = D_IN // pieces
            for s in range(pieces):
                nc.sync.dma_start(out=xr[i][:, step * s : step * (s + 1)], in_=x_view[:, i, step * s : step * (s + 1)])

        def load_w(side, c):
            wr[(side, c)] = wraw.tile([P, 4, 512], BF16, tag="wr", name="wr")
            for u in range(2):
                rows = slice(512 * c + 256 * u, 512 * c + 256 * (u + 1))
                nc.sync.dma_start(
                    out=wr[(side, c)][:, 2 * u : 2 * u + 2, :],
                    in_=W1[rows, 512 * side : 512 * (side + 1)].rearrange("(q e) w -> q e w", e=2),
                )

        def load_w2():
            nc.sync.dma_start(out=w2r[:], in_=W2.rearrange("(a p) j -> p a j", p=P))

        xg = {}

        def x_transpose(i, gp):
            u = 3 * i + gp
            bank = new_bank()
            words = xr[i][:].bitcast(F32)
            for s in range(4):
                nc.tensor.transpose(bank[:, P * s : P * (s + 1)], words[:, 512 * gp + P * s : 512 * gp + P * (s + 1)], ident_f[:])
            xg[u] = xgp.tile([P, 1024], BF16, tag="xg", name="xg", align_bytes=256)
            dst = xg[u][:].bitcast(F32).rearrange("p (g n u) -> p g n u", g=2, u=2)
            src = bank[:].rearrange("p (g u n) -> p g n u", g=2, u=2)
            if u in CO_ON_VECTOR:
                nc.vector.tensor_copy(out=dst, in_=src)
            else:
                nc.scalar.copy(out=dst, in_=src)

        def x_quantise(i, gp):
            u = 3 * i + gp
            cols = slice(P * i, P * (i + 1))
            for g2 in range(2):
                g = 2 * gp + g2
                nc.vector.quantize_mx(
                    out=xq[:, g, cols].bitcast(FP8X4), scales=xs[:, g, cols], in_=xg[u][:, 512 * g2 : 512 * (g2 + 1)]
                )

        def small_prep():
            mt = new_bank(BF16, 2 * P)
            for a in range(2):
                nc.tensor.transpose(mt[:, P * a : P * (a + 1)], misc[:, P * a : P * (a + 1)], ident_b[:])
            mview = mt[:].rearrange("p (a r) -> p a r", a=2)
            nc.vector.tensor_scalar(out=cTm2[:], in0=mview[:, :, 0:NCL], scalar1=-2.0, scalar2=None, op0=ALU.mult)
            nc.vector.tensor_copy(out=b1T[:], in_=mt[:, 32 : 32 + MT])
            nc.vector.tensor_copy(out=b2T[:], in_=mt[:, 64:66])
            nc.vector.tensor_tensor(out=csq[:], in0=cTm2[:], in1=cTm2[:], op=ALU.mult)

        def small_prep2():
            cb = new_bank()
            for a in range(2):
                nc.tensor.matmul(out=cb[:, H1 : H1 + NCL], lhsT=ones_f[:], rhs=csq[:, a, :], start=(a == 0), stop=(a == 1))
            return cb

        def small_prep3(cb):
            nc.vector.tensor_scalar(out=cc1[:], in0=cb[:, H1 : H1 + NCL], scalar1=0.25, scalar2=1.0, op0=ALU.mult, op1=ALU.add)

        wg = {}

        def regroup(engine, dst, src):
            d = dst.rearrange("p (c i) t -> p c t i", i=8)
            s = src.rearrange("p t (c i) -> p c t i", i=8)
            if engine == "v":
                nc.vector.tensor_copy(out=d, in_=s)
            else:
                nc.scalar.copy(out=d, in_=s)

        def w_regroup(side, c, quarter, engine):
            if (side, c) not in wg:
                wg[(side, c)] = wgp.tile([P, 512, 4], BF16, tag="wg", name="wg", align_bytes=256)
            cols = slice(256 * quarter, 256 * (quarter + 1))
            regroup(engine, wg[(side, c)][:, cols, :], wr[(side, c)][:, :, cols])

        def w_quantise(side, c, quarter):
            cols = slice(256 * quarter, 256 * (quarter + 1))
            dcols = slice(512 * side + 256 * quarter, 512 * side + 256 * (quarter + 1))
            nc.vector.quantize_mx(
                out=wq[:, c, dcols].bitcast(FP8X4),
                scales=ws[:, c, dcols],
                in_=wg[(side, c)][:, cols, :].rearrange("p w t -> p (w t)"),
            )

        def l1_pass(acc, m, g, col0, ncols):
            nc.tensor.matmul_mx(
                out=acc[:, 0:ncols],
                lhsT=wq[:, g, P * m : P * (m + 1)].bitcast(FP8X4),
                lhsT_scale=ws[:, g, P * m : P * (m + 1)],
                rhs=xq[:, g, col0 : col0 + ncols].bitcast(FP8X4),
                rhs_scale=xs[:, g, col0 : col0 + ncols],
                start=(g == 0),
                stop=(g == G1 - 1),
            )

        def silu(acc, m, col0, ncols):
            nc.scalar.activation(
                out=h_bf[:, m, col0 : col0 + ncols], in_=acc[:, 0:ncols], func=AF.Silu, bias=b1T[:, m : m + 1], scale=1.0
            )

        def h_quantise(col0, ncols, gg):
            hg = hgp.tile([P, 512, 4], BF16, tag="hg", name="hg", align_bytes=256)
            regroup("v", hg[:, 0:ncols, :], h_bf[:, 4 * gg : 4 * (gg + 1), col0 : col0 + ncols])
            return hg[:, 0:ncols, :]

        def h_quantise2(hg, col0, ncols, gg):
            nc.vector.quantize_mx(
                out=hq[:, gg, col0 : col0 + ncols].bitcast(FP8X4),
                scales=hs[:, gg, col0 : col0 + ncols],
                in_=hg.rearrange("p n t -> p (n t)"),
            )

        def w2_regroup(gg):
            regroup("v", w2g[:, gg, :, :], w2r[:, 4 * gg : 4 * (gg + 1), :])

        def w2_quantise():
            nc.vector.quantize_mx(
                out=w2q[:].rearrange("p g j -> p (g j)").bitcast(FP8X4),
                scales=w2s[:].rearrange("p g j -> p (g j)"),
                in_=w2g[:].rearrange("p g j t -> p (g j t)"),
            )

        def layer2(col0, ncols):
            i0, nt = col0 // P, ncols // P
            zt = []
            for jt in range(2):
                if ncols == 512 or jt == 0:
                    bank = new_bank()
                off = 0 if ncols == 512 else ncols * jt
                for gg in range(G2):
                    nc.tensor.matmul_mx(
                        out=bank[:, off : off + ncols],
                        lhsT=w2q[:, gg, P * jt : P * (jt + 1)].bitcast(FP8X4),
                        lhsT_scale=w2s[:, gg, P * jt : P * (jt + 1)],
                        rhs=hq[:, gg, col0 : col0 + ncols].bitcast(FP8X4),
                        rhs_scale=hs[:, gg, col0 : col0 + ncols],
                        start=(gg == 0),
                        stop=(gg == G2 - 1),
                    )
                zt.append(bank[:, off : off + ncols])
            for jt in range(2):
                nc.scalar.activation(
                    out=zT_sb[:, jt, col0 : col0 + ncols], in_=zt[jt], func=AF.Identity, bias=b2T[:, jt : jt + 1], scale=1.0
                )

        st = {}

        def d_pe(col0, ncols, share=None):
            i0, nt = col0 // P, ncols // P
            zb = []
            for ii in range(nt):
                if ii % 2 == 0:
                    zb.append(new_bank())
                for jt in range(2):
                    off = H1 * (ii % 2) + P * jt
                    nc.tensor.transpose(zb[-1][:, off : off + P], zT_sb[:, jt, P * (i0 + ii) : P * (i0 + ii + 1)], ident_f[:])
            db = new_bank() if share is None else st[share][1]
            slot0 = 0 if share is None else i0 - share // P
            for ii in range(nt):
                i = i0 + ii
                for jt in range(2):
                    nc.tensor.matmul(
                        out=db[:, 32 * (slot0 + ii) : 32 * (slot0 + ii) + NCL],
                        lhsT=zT_sb[:, jt, P * i : P * (i + 1)],
                        rhs=cTm2[:, jt, :],
                        start=(jt == 0),
                        stop=(jt == 1),
                    )
            st[col0] = (zb, db)

        def d_sq(col0, ncols):
            i0, nt = col0 // P, ncols // P
            zb = st[col0][0]
            for ii in range(nt):
                junk = small.tile([P, H1], F32, tag="junk", name="junk")
                nc.scalar.activation(
                    out=junk[:], in_=zb[ii // 2][:, H1 * (ii % 2) : H1 * (ii % 2 + 1)], func=AF.Square, accum_out=z2[:, i0 + ii : i0 + ii + 1]
                )

        def d_zc(col0, ncols, engine):
            i0, nt = col0 // P, ncols // P
            for k, bank in enumerate(st[col0][0]):
                n_in = min(2, nt - 2 * k)
                dst = z_sb[:, i0 + 2 * k : i0 + 2 * k + n_in, :].rearrange("p i j -> p (i j)")
                if engine == "s":
                    nc.scalar.copy(out=dst, in_=bank[:, 0 : H1 * n_in])
                else:
                    nc.vector.tensor_copy(out=dst, in_=bank[:, 0 : H1 * n_in])
            nc.sync.dma_start(out=z_view[:, i0 : i0 + nt, :], in_=z_sb[:, i0 : i0 + nt, :])

        def d_v(parts):
            work = []
            for i0, nt, db, slot0 in parts:
                shape = [P, nt, NCL]
                names = ["%s%d_%d" % (s, nt, i0) for s in ("dd", "tt", "sm", "rs")]
                dd = small.tile(shape, F32, tag=names[0], name=names[0])
                tt = small.tile(shape, F32, tag=names[1], name=names[1])
                sm = small.tile([P, nt], F32, tag=names[2], name=names[2])
                rs = small.tile([P, nt], F32, tag=names[3], name=names[3])
                dview = db[:, 32 * slot0 : 32 * (slot0 + nt)].rearrange("p (i k) -> p i k", k=32)[:, :, 0:NCL]
                work.append((i0, nt, shape, dview, dd, tt, sm, rs))
            for i0, nt, shape, dview, dd, tt, sm, rs in work:
                for ii in range(nt):
                    nc.vector.scalar_tensor_tensor(
                        out=dd[:, ii, :],
                        in0=dview[:, ii, :],
                        scalar=z2[:, i0 + ii : i0 + ii + 1],
                        in1=cc1[:],
                        op0=ALU.add,
                        op1=ALU.add,
                    )
            for i0, nt, shape, dview, dd, tt, sm, rs in work:
                nc.vector.reciprocal(out=tt[:], in_=dd[:])
            for i0, nt, shape, dview, dd, tt, sm, rs in work:
                nc.vector.reduce_sum(out=sm[:], in_=tt[:], axis=AX.X)
            for i0, nt, shape, dview, dd, tt, sm, rs in work:
                nc.vector.reciprocal(out=rs[:], in_=sm[:])
            for i0, nt, shape, dview, dd, tt, sm, rs in work:
                nc.vector.tensor_tensor(
                    out=q_sb[:, i0 : i0 + nt, :], in0=tt[:], in1=rs[:].unsqueeze(2).to_broadcast(shape), op=ALU.mult
                )
            first = parts[0][0]
            last = parts[-1][0] + parts[-1][1]
            nc.sync.dma_start(out=q_view[:, first:last, :], in_=q_sb[:, first:last, :])

        def w_rg(side, c):
            w_regroup(side, c, 0, "v")
            w_regroup(side, c, 1, "s")

        def w_q(side, c):
            w_quantise(side, c, 0)
            w_quantise(side, c, 1)

        def hq_all(col0, ncols, gg):
            hg = h_quantise(col0, ncols, gg)
            h_quantise2(hg, col0, ncols, gg)

        for i in range(XR_BUFS):
            load_x(i)
        keep_clock(WARM0)
        units = [(i, gp) for i in range(8) for gp in range(3)]
        for n, (i, gp) in enumerate(units):
            x_transpose(i, gp)
            if 2 <= n < 23:
                x_quantise(*units[n - 2])
            if gp == 2:
                if i < 7:
                    keep_clock(WARM1 if i < 6 else WARM2)
                if i + XR_BUFS < 8:
                    load_x(i + XR_BUFS)
                if i + XR_BUFS == EARLY_AFTER:
                    for c in range(N_EARLY):
                        load_w(0, c)
                if i + XR_BUFS == 7:
                    for c in range(N_EARLY, G1):
                        load_w(0, c)
                if i == 1:
                    small_prep()
                if i == 3:
                    small_prep3(small_prep2())
                if i == 6:
                    w_rg(0, 0)
            if (i, gp) == (7, 0):
                w_q(0, 0)
        x_quantise(7, 0)

        acc = {}
        for b in range(2):
            for m in range(4):
                acc[(m, b)] = new_bank()
        halves = [(side, c) for side in range(2) for c in range(G1)]
        w_rg(0, 1)
        x_quantise(7, 1)
        for c in range(G1):
            if c == 1:
                w_q(0, c)
                w_rg(*halves[c + 1])
            elif c > 1:
                w_rg(*halves[c + 1])
                w_q(0, c)
            if c == 2:
                x_quantise(7, 2)
            load_w(1, c)
            if c in (0, G1 - 1):
                order = [(m, b) for b in range(2) for m in range(4)]
            else:
                order = [(m, b) for m in range(4) for b in range(2)]
            for m, b in order:
                l1_pass(acc[(m, b)], m, c, 512 * b, 512)
        load_w2()
        for c in range(G1):
            if c == 2:
                for m in range(4):
                    silu(acc[(m, 0)], m, 0, 512)
            if c + 1 < G1:
                w_rg(1, c + 1)
            w_q(1, c)
            if c == 4:
                w2_regroup(0)
            if c == 5:
                w2_regroup(1)
        for m in range(4):
            silu(acc[(m, 1)], m, 512, 512)
        acca = {}
        for m in range(4, 8):
            acca[m] = new_bank()
        for g in range(G1):
            for m in range(4, 8):
                l1_pass(acca[m], m, g, 0, 512)
        hga0 = h_quantise(0, 512, 0)
        w2_quantise()
        hgb0 = h_quantise(512, 256, 0)
        h_quantise2(hga0, 0, 512, 0)
        hgc0 = h_quantise(768, 256, 0)
        h_quantise2(hgb0, 512, 256, 0)
        for m in range(4, 8):
            silu(acca[m], m, 0, 512)
        hga1 = h_quantise(0, 512, 1)
        h_quantise2(hgc0, 768, 256, 0)
        h_quantise2(hga1, 0, 512, 1)

        def round2(col0, ncols, ms, split=False):
            for m in ms:
                a = new_bank()
                for g in range(G1):
                    l1_pass(a, m, g, col0, ncols)
                silu(a, m, col0, ncols)
                if m == 7 and not split:
                    hq_all(col0, ncols, 1)
                if m == 7 and split:
                    ha = h_quantise(col0, 128, 1)
                    hb = h_quantise(col0 + 128, 128, 1)
                    h_quantise2(ha, col0, 128, 1)
                    h_quantise2(hb, col0 + 128, 128, 1)

        round2(512, 256, range(4, 8))
        round2(768, 256, range(4, 7))
        layer2(0, 512)
        round2(768, 256, range(7, 8), split=True)
        layer2(512, 256)
        d_pe(0, 512)
        d_sq(0, 512)
        layer2(768, 128)
        layer2(896, 128)
        d_zc(0, 512, "v")
        d_v([(0, 2, st[0][1], 0), (2, 2, st[0][1], 2)])
        d_pe(512, 256)
        d_sq(512, 256)
        d_pe(768, 128, share=512)
        d_pe(896, 128, share=512)
        d_sq(768, 128)
        d_sq(896, 128)
        d_zc(512, 256, "v")
        d_zc(768, 128, "s")
        d_zc(896, 128, "s")
        d_v([(4, 2, st[512][1], 0), (6, 2, st[512][1], 2)])
